import numpy as np
import ml_dtypes


def mxq(x, axis, fmt="e4m3"):
    dtype, down = {"e4m3": (ml_dtypes.float8_e4m3fn, 7), "e5m2": (ml_dtypes.float8_e5m2, 14)}[fmt]
    v = np.moveaxis(np.asarray(x, np.float32).astype(ml_dtypes.bfloat16).astype(np.float64), axis, -1)
    blocks = v.reshape(v.shape[:-1] + (-1, 32))
    amax = np.abs(blocks).max(-1, keepdims=True)
    byte = np.maximum(np.where(amax > 0, np.frexp(amax)[1] - 1 + 127, 0) - down, 1)
    scale = np.exp2(byte - 127.0)
    codes = (blocks / scale).astype(np.float32).astype(dtype).astype(np.float64)
    return np.moveaxis((codes * scale).reshape(v.shape), -1, axis)


WIDE = False


def mx_kscale(k):
    if not WIDE:
        return np.ones(k)
    levels = np.array([10, -10, 5, -5, 0])
    a = np.random.permutation(np.resize(levels, k // 512 * 4)).reshape(k // 512, 4)
    idx = np.arange(k)
    return np.exp2(a[idx // 512, idx % 128 // 32])


BF16 = ml_dtypes.bfloat16


def bf(x):
    return np.asarray(x, np.float32).astype(BF16)


def f64(x):
    return np.asarray(x).astype(np.float64)


B, S, D_IN, D_OUT = 2, 4096, 1024, 256


def quant8(w):
    mv = np.max(np.abs(w))
    q = np.ceil(np.log2(mv)) - 6.0
    scale = np.exp2(q)
    return np.round(w / scale) * scale


def setup_inputs():
    s = mx_kscale(D_IN)
    x = np.random.standard_normal((B, S, D_IN))
    weight = np.random.standard_normal((D_OUT, D_IN)) * 3.0 / np.sqrt(D_IN)
    w_upper = quant8(weight)
    w_lower = weight - w_upper
    return {"x": bf(x * s), "weight_upper": bf(w_upper / s[None, :]), "weight_lower": bf(w_lower / s[None, :])}


def reference(x, weight_upper, weight_lower):
    xq = mxq(f64(x), 2, "e4m3")
    y_upper = xq @ mxq(f64(weight_upper), 1, "e4m3").T
    y_lower = xq @ mxq(f64(weight_lower), 1, "e4m3").T
    return y_upper + y_lower

@@ -1,0 +1,149 @@
+from contextlib import ExitStack
+
+import concourse.mybir as mybir
+from concourse.masks import make_identity
+
+BF16 = mybir.dt.bfloat16
+F32 = mybir.dt.float32
+U32 = mybir.dt.uint32
+U8 = mybir.dt.uint8
+FP8X4 = mybir.dt.float8_e4m3fn_x4
+
+P = 128
+K = 1024
+N_OUT = 256
+TOKENS = 8192
+CHUNK = 4
+N_CHUNKS = TOKENS // (P * CHUNK)
+AHEAD = 8
+
+FLOPS = 2 * 2 * TOKENS * K * N_OUT
+
+
+def tile_virtual16bmatmul_t_kernel(tc, x, weight_upper, weight_lower, out):
+    nc = tc.nc
+    xf = x.flatten_outer_dims()
+    of = out.flatten_outer_dims()
+
+    with ExitStack() as ctx:
+        const = ctx.enter_context(tc.tile_pool(name="const", bufs=1))
+        wraw_pool = ctx.enter_context(tc.tile_pool(name="wrawp", bufs=4))
+        x_pool = ctx.enter_context(tc.tile_pool(name="xp", bufs=N_CHUNKS))
+        g_pool = ctx.enter_context(tc.tile_pool(name="gp", bufs=8))
+        c_pool = ctx.enter_context(tc.tile_pool(name="cp", bufs=12))
+        o_pool = ctx.enter_context(tc.tile_pool(name="op", bufs=6))
+        t_psum = ctx.enter_context(tc.psum_pool(name="tps", bufs=4))
+        a_psum = ctx.enter_context(tc.psum_pool(name="aps", bufs=4))
+        ctx.enter_context(tc.manual_schedule())
+
+        ident = const.tile([P, P], F32, name="ident")
+        make_identity(nc, ident[:])
+
+        w_raw = []
+        for wi, w_src in enumerate((weight_upper, weight_lower)):
+            for h in range(2):
+                wr = wraw_pool.tile([P, K], BF16, name="wraw%d" % (2 * wi + h), tag="wraw")
+                nc.sync.dma_start(out=wr[:], in_=w_src[P * h : P * (h + 1), :])
+                w_raw.append(wr)
+
+        x_chunks = {}
+
+        def load_chunk(c, pieces):
+            xc = x_pool.tile([P, CHUNK * K], BF16, name="xc%d" % c, tag="xc")
+            src = xf[CHUNK * P * c : CHUNK * P * (c + 1), :].rearrange("(p t) k -> p (t k)", t=CHUNK)
+            step = CHUNK * K // pieces
+            for i in range(pieces):
+                nc.sync.dma_start(out=xc[:, step * i : step * (i + 1)], in_=src[:, step * i : step * (i + 1)])
+            x_chunks[c] = xc
+
+        load_chunk(0, 4)
+        load_chunk(1, 2)
+        for c in range(2, AHEAD):
+            load_chunk(c, 1)
+
+        def transpose_words(bank, words):
+            for c in range(4):
+                nc.tensor.transpose(bank[:, c, :], words[:, P * c : P * (c + 1)], ident[:])
+
+        w_codes = []
+        w_scales = []
+        for wi in range(2):
+            wg = const.tile([P, 4 * 2 * N_OUT], BF16, name="wg%d" % wi, align_bytes=64)
+            wg_words = wg[:].bitcast(F32).rearrange("p (g n u) -> p g n u", g=2, u=2)
+            for h in range(2):
+                wt = a_psum.tile([P, 4, P], F32, name="wt%d" % (2 * wi + h), tag="acc")
+                transpose_words(wt, w_raw[2 * wi + h][:].bitcast(F32))
+                nc.scalar.copy(
+                    out=wg_words[:, :, P * h : P * (h + 1), :],
+                    in_=wt[:].rearrange("p (g u) r -> p g r u", u=2),
+                )
+            wc = const.tile([P, 2 * N_OUT], U32, name="wc%d" % wi, align_bytes=64)
+            ws = const.tile([P, 2 * N_OUT], U8, name="ws%d" % wi, align_bytes=64)
+            nc.vector.quantize_mx(out=wc[:].bitcast(FP8X4), scales=ws[:], in_=wg[:])
+            w_codes.append(wc)
+            w_scales.append(ws)
+
+        x_codes = {}
+        x_scales = {}
+        acc = {}
+        o_tiles = {}
+
+        def prepare(group):
+            grouped = {}
+            for i in group:
+                words = x_chunks[i // CHUNK][:].bitcast(F32)
+                t = i % CHUNK
+                xt = t_psum.tile([P, 4, P], F32, name="xt%d" % i, tag="xt")
+                transpose_words(xt, words[:, (K // 2) * t : (K // 2) * (t + 1)])
+                gr = g_pool.tile([P, K], BF16, name="gr%d" % i, tag="gr", align_bytes=64)
+                nc.scalar.copy(
+                    out=gr[:].bitcast(F32).rearrange("p (g r u) -> p g r u", g=2, u=2),
+                    in_=xt[:].rearrange("p (g u) r -> p g r u", u=2),
+                )
+                grouped[i] = gr
+            for i in group:
+                xcod = c_pool.tile([P, K // 4], U32, name="xcod%d" % i, tag="xcod", align_bytes=64)
+                xsca = c_pool.tile([P, K // 4], U8, name="xsca%d" % i, tag="xsca", align_bytes=64)
+                nc.vector.quantize_mx(out=xcod[:].bitcast(FP8X4), scales=xsca[:], in_=grouped[i][:])
+                x_codes[i] = xcod
+                x_scales[i] = xsca
+
+        def multiply(group):
+            for i in group:
+                pair = i // 2
+                c = i // CHUNK
+                if i % 2 == 0:
+                    acc[pair] = a_psum.tile([P, 2, N_OUT], F32, name="acc%d" % pair, tag="acc")
+                if i % CHUNK == 0:
+                    o_tiles[c] = o_pool.tile([P, CHUNK * N_OUT], F32, name="osb%d" % c, tag="osb")
+                n_pass = 0
+                for g in range(2):
+                    for wi in range(2):
+                        nc.tensor.matmul_mx(
+                            out=acc[pair][:, i % 2, :],
+                            lhsT=x_codes[i][:, P * g : P * (g + 1)].bitcast(FP8X4),
+                            lhsT_scale=x_scales[i][:, P * g : P * (g + 1)],
+                            rhs=w_codes[wi][:, N_OUT * g : N_OUT * (g + 1)].bitcast(FP8X4),
+                            rhs_scale=w_scales[wi][:, N_OUT * g : N_OUT * (g + 1)],
+                            start=(n_pass == 0),
+                            stop=(n_pass == 3),
+                        )
+                        n_pass += 1
+                if i % 2 == 1:
+                    b = pair % 2
+                    cols = slice(2 * N_OUT * b, 2 * N_OUT * (b + 1))
+                    nc.vector.tensor_copy(out=o_tiles[c][:, cols], in_=acc[pair][:].rearrange("p h n -> p (h n)"))
+                    dst = of[CHUNK * P * c : CHUNK * P * (c + 1), :].rearrange("(p t) n -> p (t n)", t=CHUNK)
+                    if c == N_CHUNKS - 1:
+                        nc.sync.dma_start(out=dst[:, cols], in_=o_tiles[c][:, cols])
+                    elif b == 1:
+                        nc.sync.dma_start(out=dst, in_=o_tiles[c][:])
+                        if c + AHEAD < N_CHUNKS:
+                            load_chunk(c + AHEAD, 1)
+
+        groups = [[0], [1], [2, 3]] + [list(range(CHUNK * c, CHUNK * (c + 1))) for c in range(1, N_CHUNKS)]
+        prepare(groups[0])
+        for k in range(len(groups)):
+            if k + 1 < len(groups):
+                prepare(groups[k + 1])
+            multiply(groups[k])

@@ -61,6 +61,16 @@ def tile_virtual16bmatmul_t_kernel(tc, x, weight_upper, weight_lower, out):
         for c in range(2, AHEAD):
             load_chunk(c, 1)
 
+        warm_src = const.tile([P, 512], BF16, name="warm_src")
+        nc.vector.memset(warm_src[:], 0.0)
+        warm_bank = a_psum.tile([P, 512], F32, name="warm_bank", tag="acc")
+
+        def keep_warm(n):
+            for rep in range(n):
+                nc.tensor.matmul(out=warm_bank[:], lhsT=warm_src[:, 0:P], rhs=warm_src[:], start=True, stop=True)
+
+        keep_warm(6)
+
         def transpose_words(bank, words):
             for c in range(4):
                 nc.tensor.transpose(bank[:, c, :], words[:, P * c : P * (c + 1)], ident[:])
@@ -71,8 +81,9 @@ def tile_virtual16bmatmul_t_kernel(tc, x, weight_upper, weight_lower, out):
             wg = const.tile([P, 4 * 2 * N_OUT], BF16, name="wg%d" % wi, align_bytes=64)
             wg_words = wg[:].bitcast(F32).rearrange("p (g n u) -> p g n u", g=2, u=2)
             for h in range(2):
-                wt = a_psum.tile([P, 4, P], F32, name="wt%d" % (2 * wi + h), tag="acc")
+                wt = t_psum.tile([P, 4, P], F32, name="wt%d" % (2 * wi + h), tag="xt")
                 transpose_words(wt, w_raw[2 * wi + h][:].bitcast(F32))
+                keep_warm(1)
                 nc.scalar.copy(
                     out=wg_words[:, :, P * h : P * (h + 1), :],
                     in_=wt[:].rearrange("p (g u) r -> p g r u", u=2),
@@ -95,6 +106,8 @@ def tile_virtual16bmatmul_t_kernel(tc, x, weight_upper, weight_lower, out):
                 t = i % CHUNK
                 xt = t_psum.tile([P, 4, P], F32, name="xt%d" % i, tag="xt")
                 transpose_words(xt, words[:, (K // 2) * t : (K // 2) * (t + 1)])
+                if i < 2:
+                    keep_warm(1)
                 gr = g_pool.tile([P, K], BF16, name="gr%d" % i, tag="gr", align_bytes=64)
                 nc.scalar.copy(
                     out=gr[:].bitcast(F32).rearrange("p (g r u) -> p g r u", g=2, u=2),

@@ -13,9 +13,14 @@ P = 128
 K = 1024
 N_OUT = 256
 TOKENS = 8192
+N_TILES = TOKENS // P
 CHUNK = 4
-N_CHUNKS = TOKENS // (P * CHUNK)
+N_CHUNKS = N_TILES // CHUNK
 AHEAD = 8
+GROUP = 6
+T_BUFS = 6
+A_BUFS = 2
+EARLY_Q = 4
 
 FLOPS = 2 * 2 * TOKENS * K * N_OUT
 
@@ -30,10 +35,10 @@ def tile_virtual16bmatmul_t_kernel(tc, x, weight_upper, weight_lower, out):
         wraw_pool = ctx.enter_context(tc.tile_pool(name="wrawp", bufs=4))
         x_pool = ctx.enter_context(tc.tile_pool(name="xp", bufs=N_CHUNKS))
         g_pool = ctx.enter_context(tc.tile_pool(name="gp", bufs=8))
-        c_pool = ctx.enter_context(tc.tile_pool(name="cp", bufs=12))
+        c_pool = ctx.enter_context(tc.tile_pool(name="cp", bufs=16))
         o_pool = ctx.enter_context(tc.tile_pool(name="op", bufs=6))
-        t_psum = ctx.enter_context(tc.psum_pool(name="tps", bufs=4))
-        a_psum = ctx.enter_context(tc.psum_pool(name="aps", bufs=4))
+        t_psum = ctx.enter_context(tc.psum_pool(name="tps", bufs=T_BUFS))
+        a_psum = ctx.enter_context(tc.psum_pool(name="aps", bufs=A_BUFS))
         ctx.enter_context(tc.manual_schedule())
 
         ident = const.tile([P, P], F32, name="ident")
@@ -63,7 +68,7 @@ def tile_virtual16bmatmul_t_kernel(tc, x, weight_upper, weight_lower, out):
 
         warm_src = const.tile([P, 512], BF16, name="warm_src")
         nc.vector.memset(warm_src[:], 0.0)
-        warm_bank = a_psum.tile([P, 512], F32, name="warm_bank", tag="acc")
+        warm_bank = t_psum.tile([P, 512], F32, name="warm_bank", tag="xt")
 
         def keep_warm(n):
             for rep in range(n):
@@ -94,69 +99,82 @@ def tile_virtual16bmatmul_t_kernel(tc, x, weight_upper, weight_lower, out):
             w_codes.append(wc)
             w_scales.append(ws)
 
+        grouped = {}
         x_codes = {}
         x_scales = {}
         acc = {}
         o_tiles = {}
 
-        def prepare(group):
-            grouped = {}
-            for i in group:
-                words = x_chunks[i // CHUNK][:].bitcast(F32)
-                t = i % CHUNK
-                xt = t_psum.tile([P, 4, P], F32, name="xt%d" % i, tag="xt")
-                transpose_words(xt, words[:, (K // 2) * t : (K // 2) * (t + 1)])
-                if i < 2:
-                    keep_warm(1)
-                gr = g_pool.tile([P, K], BF16, name="gr%d" % i, tag="gr", align_bytes=64)
-                nc.scalar.copy(
-                    out=gr[:].bitcast(F32).rearrange("p (g r u) -> p g r u", g=2, u=2),
-                    in_=xt[:].rearrange("p (g u) r -> p g r u", u=2),
-                )
-                grouped[i] = gr
-            for i in group:
-                xcod = c_pool.tile([P, K // 4], U32, name="xcod%d" % i, tag="xcod", align_bytes=64)
-                xsca = c_pool.tile([P, K // 4], U8, name="xsca%d" % i, tag="xsca", align_bytes=64)
-                nc.vector.quantize_mx(out=xcod[:].bitcast(FP8X4), scales=xsca[:], in_=grouped[i][:])
-                x_codes[i] = xcod
-                x_scales[i] = xsca
+        def transpose_tile(i):
+            words = x_chunks[i // CHUNK][:].bitcast(F32)
+            t = i % CHUNK
+            xt = t_psum.tile([P, 4, P], F32, name="xt%d" % i, tag="xt")
+            transpose_words(xt, words[:, (K // 2) * t : (K // 2) * (t + 1)])
+            if i < 2:
+                keep_warm(1)
+            gr = g_pool.tile([P, K], BF16, name="gr%d" % i, tag="gr", align_bytes=64)
+            nc.scalar.copy(
+                out=gr[:].bitcast(F32).rearrange("p (g r u) -> p g r u", g=2, u=2),
+                in_=xt[:].rearrange("p (g u) r -> p g r u", u=2),
+            )
+            grouped[i] = gr
 
-        def multiply(group):
-            for i in group:
-                pair = i // 2
-                c = i // CHUNK
-                if i % 2 == 0:
-                    acc[pair] = a_psum.tile([P, 2, N_OUT], F32, name="acc%d" % pair, tag="acc")
-                if i % CHUNK == 0:
-                    o_tiles[c] = o_pool.tile([P, CHUNK * N_OUT], F32, name="osb%d" % c, tag="osb")
-                n_pass = 0
-                for g in range(2):
-                    for wi in range(2):
-                        nc.tensor.matmul_mx(
-                            out=acc[pair][:, i % 2, :],
-                            lhsT=x_codes[i][:, P * g : P * (g + 1)].bitcast(FP8X4),
-                            lhsT_scale=x_scales[i][:, P * g : P * (g + 1)],
-                            rhs=w_codes[wi][:, N_OUT * g : N_OUT * (g + 1)].bitcast(FP8X4),
-                            rhs_scale=w_scales[wi][:, N_OUT * g : N_OUT * (g + 1)],
-                            start=(n_pass == 0),
-                            stop=(n_pass == 3),
-                        )
-                        n_pass += 1
-                if i % 2 == 1:
-                    b = pair % 2
-                    cols = slice(2 * N_OUT * b, 2 * N_OUT * (b + 1))
-                    nc.vector.tensor_copy(out=o_tiles[c][:, cols], in_=acc[pair][:].rearrange("p h n -> p (h n)"))
-                    dst = of[CHUNK * P * c : CHUNK * P * (c + 1), :].rearrange("(p t) n -> p (t n)", t=CHUNK)
-                    if c == N_CHUNKS - 1:
-                        nc.sync.dma_start(out=dst[:, cols], in_=o_tiles[c][:, cols])
-                    elif b == 1:
-                        nc.sync.dma_start(out=dst, in_=o_tiles[c][:])
-                        if c + AHEAD < N_CHUNKS:
-                            load_chunk(c + AHEAD, 1)
+        def quantise_tile(i):
+            xcod = c_pool.tile([P, K // 4], U32, name="xcod%d" % i, tag="xcod", align_bytes=64)
+            xsca = c_pool.tile([P, K // 4], U8, name="xsca%d" % i, tag="xsca", align_bytes=64)
+            nc.vector.quantize_mx(out=xcod[:].bitcast(FP8X4), scales=xsca[:], in_=grouped[i][:])
+            x_codes[i] = xcod
+            x_scales[i] = xsca
 
-        groups = [[0], [1], [2, 3]] + [list(range(CHUNK * c, CHUNK * (c + 1))) for c in range(1, N_CHUNKS)]
-        prepare(groups[0])
+        def multiply_tile(i):
+            pair = i // 2
+            c = i // CHUNK
+            if i % 2 == 0:
+                acc[pair] = a_psum.tile([P, 2, N_OUT], F32, name="acc%d" % pair, tag="acc")
+            if i % CHUNK == 0:
+                o_tiles[c] = o_pool.tile([P, CHUNK * N_OUT], F32, name="osb%d" % c, tag="osb")
+            n_pass = 0
+            for g in range(2):
+                for wi in range(2):
+                    nc.tensor.matmul_mx(
+                        out=acc[pair][:, i % 2, :],
+                        lhsT=x_codes[i][:, P * g : P * (g + 1)].bitcast(FP8X4),
+                        lhsT_scale=x_scales[i][:, P * g : P * (g + 1)],
+                        rhs=w_codes[wi][:, N_OUT * g : N_OUT * (g + 1)].bitcast(FP8X4),
+                        rhs_scale=w_scales[wi][:, N_OUT * g : N_OUT * (g + 1)],
+                        start=(n_pass == 0),
+                        stop=(n_pass == 3),
+                    )
+                    n_pass += 1
+            if i % 2 == 1:
+                b = pair % 2
+                cols = slice(2 * N_OUT * b, 2 * N_OUT * (b + 1))
+                nc.vector.tensor_copy(out=o_tiles[c][:, cols], in_=acc[pair][:].rearrange("p h n -> p (h n)"))
+                dst = of[CHUNK * P * c : CHUNK * P * (c + 1), :].rearrange("(p t) n -> p (t n)", t=CHUNK)
+                if c == N_CHUNKS - 1:
+                    nc.sync.dma_start(out=dst[:, cols], in_=o_tiles[c][:, cols])
+                elif b == 1:
+                    nc.sync.dma_start(out=dst, in_=o_tiles[c][:])
+                    if c + AHEAD < N_CHUNKS:
+                        load_chunk(c + AHEAD, 1)
+
+        groups = [[0], [1], [2, 3]] + [list(range(s, s + GROUP)) for s in range(4, N_TILES, GROUP)]
+        for i in groups[0]:
+            transpose_tile(i)
+        for i in groups[0]:
+            quantise_tile(i)
         for k in range(len(groups)):
-            if k + 1 < len(groups):
-                prepare(groups[k + 1])
-            multiply(groups[k])
+            following = groups[k + 1] if k + 1 < len(groups) else []
+            for i in following:
+                transpose_tile(i)
+            for i in following[:EARLY_Q]:
+                quantise_tile(i)
+            late = following[EARLY_Q:]
+            for n, i in enumerate(groups[k]):
+                multiply_tile(i)
+                if n == 1:
+                    for j in late:
+                        quantise_tile(j)
+            if len(groups[k]) < 2:
+                for j in late:
+                    quantise_tile(j)

@@ -17,9 +17,9 @@ N_TILES = TOKENS // P
 CHUNK = 4
 N_CHUNKS = N_TILES // CHUNK
 AHEAD = 8
-GROUP = 6
-T_BUFS = 6
-A_BUFS = 2
+GROUP = 4
+T_BUFS = 4
+A_BUFS = 4
 EARLY_Q = 4
 
 FLOPS = 2 * 2 * TOKENS * K * N_OUT
@@ -68,7 +68,7 @@ def tile_virtual16bmatmul_t_kernel(tc, x, weight_upper, weight_lower, out):
 
         warm_src = const.tile([P, 512], BF16, name="warm_src")
         nc.vector.memset(warm_src[:], 0.0)
-        warm_bank = t_psum.tile([P, 512], F32, name="warm_bank", tag="xt")
+        warm_bank = a_psum.tile([P, 512], F32, name="warm_bank", tag="acc")
 
         def keep_warm(n):
             for rep in range(n):
@@ -110,7 +110,7 @@ def tile_virtual16bmatmul_t_kernel(tc, x, weight_upper, weight_lower, out):
             t = i % CHUNK
             xt = t_psum.tile([P, 4, P], F32, name="xt%d" % i, tag="xt")
             transpose_words(xt, words[:, (K // 2) * t : (K // 2) * (t + 1)])
-            if i < 2:
+            if i < 3:
                 keep_warm(1)
             gr = g_pool.tile([P, K], BF16, name="gr%d" % i, tag="gr", align_bytes=64)
             nc.scalar.copy(
@@ -129,15 +129,16 @@ def tile_virtual16bmatmul_t_kernel(tc, x, weight_upper, weight_lower, out):
         def multiply_tile(i):
             pair = i // 2
             c = i // CHUNK
-            if i % 2 == 0:
-                acc[pair] = a_psum.tile([P, 2, N_OUT], F32, name="acc%d" % pair, tag="acc")
+            alone = i >= N_TILES - 2
+            if i % 2 == 0 or alone:
+                acc[pair] = a_psum.tile([P, 2, N_OUT], F32, name="acc%d" % i, tag="acc")
             if i % CHUNK == 0:
                 o_tiles[c] = o_pool.tile([P, CHUNK * N_OUT], F32, name="osb%d" % c, tag="osb")
             n_pass = 0
             for g in range(2):
                 for wi in range(2):
                     nc.tensor.matmul_mx(
-                        out=acc[pair][:, i % 2, :],
+                        out=acc[pair][:, 0 if alone else i % 2, :],
                         lhsT=x_codes[i][:, P * g : P * (g + 1)].bitcast(FP8X4),
                         lhsT_scale=x_scales[i][:, P * g : P * (g + 1)],
                         rhs=w_codes[wi][:, N_OUT * g : N_OUT * (g + 1)].bitcast(FP8X4),
@@ -146,11 +147,18 @@ def tile_virtual16bmatmul_t_kernel(tc, x, weight_upper, weight_lower, out):
                         stop=(n_pass == 3),
                     )
                     n_pass += 1
-            if i % 2 == 1:
+            dst = of[CHUNK * P * c : CHUNK * P * (c + 1), :].rearrange("(p t) n -> p (t n)", t=CHUNK)
+            if alone:
+                cols = slice(N_OUT * (i % CHUNK), N_OUT * (i % CHUNK + 1))
+                if i % 2 == 0:
+                    nc.scalar.copy(out=o_tiles[c][:, cols], in_=acc[pair][:, 0, :])
+                else:
+                    nc.vector.tensor_copy(out=o_tiles[c][:, cols], in_=acc[pair][:, 0, :])
+                nc.sync.dma_start(out=dst[:, cols], in_=o_tiles[c][:, cols])
+            elif i % 2 == 1:
                 b = pair % 2
                 cols = slice(2 * N_OUT * b, 2 * N_OUT * (b + 1))
                 nc.vector.tensor_copy(out=o_tiles[c][:, cols], in_=acc[pair][:].rearrange("p h n -> p (h n)"))
-                dst = of[CHUNK * P * c : CHUNK * P * (c + 1), :].rearrange("(p t) n -> p (t n)", t=CHUNK)
                 if c == N_CHUNKS - 1:
                     nc.sync.dma_start(out=dst[:, cols], in_=o_tiles[c][:, cols])
                 elif b == 1:
@@ -158,7 +166,7 @@ def tile_virtual16bmatmul_t_kernel(tc, x, weight_upper, weight_lower, out):
                     if c + AHEAD < N_CHUNKS:
                         load_chunk(c + AHEAD, 1)
 
-        groups = [[0], [1], [2, 3]] + [list(range(s, s + GROUP)) for s in range(4, N_TILES, GROUP)]
+        groups = [[0, 1], [2, 3]] + [list(range(s, s + GROUP)) for s in range(4, N_TILES, GROUP)]
         for i in groups[0]:
             transpose_tile(i)
         for i in groups[0]:

@@ -11,16 +11,18 @@ FP8X4 = mybir.dt.float8_e4m3fn_x4
 
 P = 128
 K = 1024
+K_WORDS = K // 2
+PASSES = K // (4 * P)
 N_OUT = 256
 TOKENS = 8192
 N_TILES = TOKENS // P
 CHUNK = 4
 N_CHUNKS = N_TILES // CHUNK
+ROUND = 4
 AHEAD = 8
-GROUP = 4
-T_BUFS = 4
-A_BUFS = 4
-EARLY_Q = 4
+WARM_COLS = 512
+WARM_FIRST = 6
+WARM_TILES = 3
 
 FLOPS = 2 * 2 * TOKENS * K * N_OUT
 
@@ -34,12 +36,22 @@ def tile_virtual16bmatmul_t_kernel(tc, x, weight_upper, weight_lower, out):
         const = ctx.enter_context(tc.tile_pool(name="const", bufs=1))
         wraw_pool = ctx.enter_context(tc.tile_pool(name="wrawp", bufs=4))
         x_pool = ctx.enter_context(tc.tile_pool(name="xp", bufs=N_CHUNKS))
-        g_pool = ctx.enter_context(tc.tile_pool(name="gp", bufs=8))
-        c_pool = ctx.enter_context(tc.tile_pool(name="cp", bufs=16))
+        g_pool = ctx.enter_context(tc.tile_pool(name="gp", bufs=2 * ROUND))
+        c_pool = ctx.enter_context(tc.tile_pool(name="cp", bufs=4 * ROUND))
         o_pool = ctx.enter_context(tc.tile_pool(name="op", bufs=6))
-        t_psum = ctx.enter_context(tc.psum_pool(name="tps", bufs=T_BUFS))
-        a_psum = ctx.enter_context(tc.psum_pool(name="aps", bufs=A_BUFS))
+        t_psum = ctx.enter_context(tc.psum_pool(name="tps", bufs=1))
+        a_psum = ctx.enter_context(tc.psum_pool(name="aps", bufs=4))
         ctx.enter_context(tc.manual_schedule())
+
+        rounds = [[0, 1], [2, 3]] + [list(range(s, s + ROUND)) for s in range(CHUNK, N_TILES, ROUND)]
+
+        queue = [0, 1, 2, 3]
+        bank_of = {}
+        for run in [["w0"], ["w1"], ["w2"], ["w3"]] + rounds:
+            taken = list(reversed(queue[: len(run)]))
+            queue = queue[len(run) :] + taken
+            for item, bank in zip(run, taken):
+                bank_of[item] = bank
 
         ident = const.tile([P, P], F32, name="ident")
         make_identity(nc, ident[:])
@@ -66,15 +78,15 @@ def tile_virtual16bmatmul_t_kernel(tc, x, weight_upper, weight_lower, out):
         for c in range(2, AHEAD):
             load_chunk(c, 1)
 
-        warm_src = const.tile([P, 512], BF16, name="warm_src")
+        warm_src = const.tile([P, WARM_COLS], BF16, name="warm_src")
         nc.vector.memset(warm_src[:], 0.0)
-        warm_bank = a_psum.tile([P, 512], F32, name="warm_bank", tag="acc")
+        warm_bank = a_psum.tile([P, WARM_COLS], F32, name="warm_bank", tag="acc")
 
         def keep_warm(n):
             for rep in range(n):
                 nc.tensor.matmul(out=warm_bank[:], lhsT=warm_src[:, 0:P], rhs=warm_src[:], start=True, stop=True)
 
-        keep_warm(6)
+        keep_warm(WARM_FIRST)
 
         def transpose_words(bank, words):
             for c in range(4):
@@ -83,18 +95,18 @@ def tile_virtual16bmatmul_t_kernel(tc, x, weight_upper, weight_lower, out):
         w_codes = []
         w_scales = []
         for wi in range(2):
-            wg = const.tile([P, 4 * 2 * N_OUT], BF16, name="wg%d" % wi, align_bytes=64)
-            wg_words = wg[:].bitcast(F32).rearrange("p (g n u) -> p g n u", g=2, u=2)
+            wg = const.tile([P, 4 * PASSES * N_OUT], BF16, name="wg%d" % wi, align_bytes=64)
+            wg_words = wg[:].bitcast(F32).rearrange("p (g n u) -> p g n u", g=PASSES, u=2)
             for h in range(2):
-                wt = t_psum.tile([P, 4, P], F32, name="wt%d" % (2 * wi + h), tag="xt")
+                wt = t_psum.tile([P, 4, P], F32, name="wt%d" % (2 * wi + h), tag="tb%d" % bank_of["w%d" % (2 * wi + h)])
                 transpose_words(wt, w_raw[2 * wi + h][:].bitcast(F32))
                 keep_warm(1)
                 nc.scalar.copy(
                     out=wg_words[:, :, P * h : P * (h + 1), :],
                     in_=wt[:].rearrange("p (g u) r -> p g r u", u=2),
                 )
-            wc = const.tile([P, 2 * N_OUT], U32, name="wc%d" % wi, align_bytes=64)
-            ws = const.tile([P, 2 * N_OUT], U8, name="ws%d" % wi, align_bytes=64)
+            wc = const.tile([P, PASSES * N_OUT], U32, name="wc%d" % wi, align_bytes=64)
+            ws = const.tile([P, PASSES * N_OUT], U8, name="ws%d" % wi, align_bytes=64)
             nc.vector.quantize_mx(out=wc[:].bitcast(FP8X4), scales=ws[:], in_=wg[:])
             w_codes.append(wc)
             w_scales.append(ws)
@@ -108,13 +120,13 @@ def tile_virtual16bmatmul_t_kernel(tc, x, weight_upper, weight_lower, out):
         def transpose_tile(i):
             words = x_chunks[i // CHUNK][:].bitcast(F32)
             t = i % CHUNK
-            xt = t_psum.tile([P, 4, P], F32, name="xt%d" % i, tag="xt")
-            transpose_words(xt, words[:, (K // 2) * t : (K // 2) * (t + 1)])
-            if i < 3:
+            xt = t_psum.tile([P, 4, P], F32, name="xt%d" % i, tag="tb%d" % bank_of[i])
+            transpose_words(xt, words[:, K_WORDS * t : K_WORDS * (t + 1)])
+            if i < WARM_TILES:
                 keep_warm(1)
             gr = g_pool.tile([P, K], BF16, name="gr%d" % i, tag="gr", align_bytes=64)
             nc.scalar.copy(
-                out=gr[:].bitcast(F32).rearrange("p (g r u) -> p g r u", g=2, u=2),
+                out=gr[:].bitcast(F32).rearrange("p (g r u) -> p g r u", g=PASSES, u=2),
                 in_=xt[:].rearrange("p (g u) r -> p g r u", u=2),
             )
             grouped[i] = gr
@@ -126,63 +138,56 @@ def tile_virtual16bmatmul_t_kernel(tc, x, weight_upper, weight_lower, out):
             x_codes[i] = xcod
             x_scales[i] = xsca
 
-        def multiply_tile(i):
-            pair = i // 2
-            c = i // CHUNK
-            alone = i >= N_TILES - 2
-            if i % 2 == 0 or alone:
-                acc[pair] = a_psum.tile([P, 2, N_OUT], F32, name="acc%d" % i, tag="acc")
-            if i % CHUNK == 0:
-                o_tiles[c] = o_pool.tile([P, CHUNK * N_OUT], F32, name="osb%d" % c, tag="osb")
-            n_pass = 0
-            for g in range(2):
-                for wi in range(2):
-                    nc.tensor.matmul_mx(
-                        out=acc[pair][:, 0 if alone else i % 2, :],
-                        lhsT=x_codes[i][:, P * g : P * (g + 1)].bitcast(FP8X4),
-                        lhsT_scale=x_scales[i][:, P * g : P * (g + 1)],
-                        rhs=w_codes[wi][:, N_OUT * g : N_OUT * (g + 1)].bitcast(FP8X4),
-                        rhs_scale=w_scales[wi][:, N_OUT * g : N_OUT * (g + 1)],
-                        start=(n_pass == 0),
-                        stop=(n_pass == 3),
-                    )
-                    n_pass += 1
-            dst = of[CHUNK * P * c : CHUNK * P * (c + 1), :].rearrange("(p t) n -> p (t n)", t=CHUNK)
-            if alone:
-                cols = slice(N_OUT * (i % CHUNK), N_OUT * (i % CHUNK + 1))
-                if i % 2 == 0:
-                    nc.scalar.copy(out=o_tiles[c][:, cols], in_=acc[pair][:, 0, :])
-                else:
-                    nc.vector.tensor_copy(out=o_tiles[c][:, cols], in_=acc[pair][:, 0, :])
-                nc.sync.dma_start(out=dst[:, cols], in_=o_tiles[c][:, cols])
-            elif i % 2 == 1:
-                b = pair % 2
-                cols = slice(2 * N_OUT * b, 2 * N_OUT * (b + 1))
-                nc.vector.tensor_copy(out=o_tiles[c][:, cols], in_=acc[pair][:].rearrange("p h n -> p (h n)"))
-                if c == N_CHUNKS - 1:
-                    nc.sync.dma_start(out=dst[:, cols], in_=o_tiles[c][:, cols])
-                elif b == 1:
-                    nc.sync.dma_start(out=dst, in_=o_tiles[c][:])
-                    if c + AHEAD < N_CHUNKS:
-                        load_chunk(c + AHEAD, 1)
+        drained = {}
 
-        groups = [[0, 1], [2, 3]] + [list(range(s, s + GROUP)) for s in range(4, N_TILES, GROUP)]
-        for i in groups[0]:
-            transpose_tile(i)
-        for i in groups[0]:
-            quantise_tile(i)
-        for k in range(len(groups)):
-            following = groups[k + 1] if k + 1 < len(groups) else []
-            for i in following:
-                transpose_tile(i)
-            for i in following[:EARLY_Q]:
-                quantise_tile(i)
-            late = following[EARLY_Q:]
-            for n, i in enumerate(groups[k]):
-                multiply_tile(i)
-                if n == 1:
-                    for j in late:
-                        quantise_tile(j)
-            if len(groups[k]) < 2:
-                for j in late:
-                    quantise_tile(j)
+        def multiply_round(order, last):
+            for n, i in enumerate(order):
+                c = i // CHUNK
+                alone = last and n >= len(order) - 2
+                if n % 2 == 0 or alone:
+                    acc[0] = a_psum.tile([P, 2, N_OUT], F32, name="acc%d" % i, tag="acc")
+                if c not in o_tiles:
+                    o_tiles[c] = o_pool.tile([P, CHUNK * N_OUT], F32, name="osb%d" % c, tag="osb")
+                    drained[c] = 0
+                n_pass = 0
+                for g in range(PASSES):
+                    for wi in range(2):
+                        nc.tensor.matmul_mx(
+                            out=acc[0][:, 0 if alone else i % 2, :],
+                            lhsT=x_codes[i][:, P * g : P * (g + 1)].bitcast(FP8X4),
+                            lhsT_scale=x_scales[i][:, P * g : P * (g + 1)],
+                            rhs=w_codes[wi][:, N_OUT * g : N_OUT * (g + 1)].bitcast(FP8X4),
+                            rhs_scale=w_scales[wi][:, N_OUT * g : N_OUT * (g + 1)],
+                            start=(n_pass == 0),
+                            stop=(n_pass == 2 * PASSES - 1),
+                        )
+                        n_pass += 1
+                dst = of[CHUNK * P * c : CHUNK * P * (c + 1), :].rearrange("(p t) n -> p (t n)", t=CHUNK)
+                if alone:
+                    cols = slice(N_OUT * (i % CHUNK), N_OUT * (i % CHUNK + 1))
+                    if n == len(order) - 2:
+                        nc.scalar.copy(out=o_tiles[c][:, cols], in_=acc[0][:, 0, :])
+                    else:
+                        nc.vector.tensor_copy(out=o_tiles[c][:, cols], in_=acc[0][:, 0, :])
+                    nc.sync.dma_start(out=dst[:, cols], in_=o_tiles[c][:, cols])
+                elif n % 2 == 1:
+                    b = (i // 2) % 2
+                    cols = slice(2 * N_OUT * b, 2 * N_OUT * (b + 1))
+                    nc.vector.tensor_copy(out=o_tiles[c][:, cols], in_=acc[0][:].rearrange("p h n -> p (h n)"))
+                    drained[c] += 1
+                    if last:
+                        nc.sync.dma_start(out=dst[:, cols], in_=o_tiles[c][:, cols])
+                    elif drained[c] == 2:
+                        nc.sync.dma_start(out=dst, in_=o_tiles[c][:])
+                        if c + AHEAD < N_CHUNKS:
+                            load_chunk(c + AHEAD, 1)
+
+        for k in range(-1, len(rounds)):
+            if k + 1 < len(rounds):
+                for i in rounds[k + 1]:
+                    transpose_tile(i)
+                for i in rounds[k + 1]:
+                    quantise_tile(i)
+            if k >= 0:
+                order = rounds[k] if k < 2 else list(reversed(rounds[k]))
+                multiply_round(order, k == len(rounds) - 1)

from contextlib import ExitStack

import concourse.mybir as mybir
from concourse.masks import make_identity

BF16 = mybir.dt.bfloat16
F32 = mybir.dt.float32
U32 = mybir.dt.uint32
U8 = mybir.dt.uint8
FP8X4 = mybir.dt.float8_e4m3fn_x4

P = 128
K = 1024
K_WORDS = K // 2
PASSES = K // (4 * P)
N_OUT = 256
TOKENS = 8192
N_TILES = TOKENS // P
CHUNK = 4
N_CHUNKS = N_TILES // CHUNK
ROUND = 4
AHEAD = 8
WARM_COLS = 512
WARM_FIRST = 6
WARM_TILES = 3

FLOPS = 2 * 2 * TOKENS * K * N_OUT


def tile_virtual16bmatmul_t_kernel(tc, x, weight_upper, weight_lower, out):
    nc = tc.nc
    xf = x.flatten_outer_dims()
    of = out.flatten_outer_dims()

    with ExitStack() as ctx:
        const = ctx.enter_context(tc.tile_pool(name="const", bufs=1))
        wraw_pool = ctx.enter_context(tc.tile_pool(name="wrawp", bufs=4))
        x_pool = ctx.enter_context(tc.tile_pool(name="xp", bufs=N_CHUNKS))
        g_pool = ctx.enter_context(tc.tile_pool(name="gp", bufs=2 * ROUND))
        c_pool = ctx.enter_context(tc.tile_pool(name="cp", bufs=4 * ROUND))
        o_pool = ctx.enter_context(tc.tile_pool(name="op", bufs=6))
        t_psum = ctx.enter_context(tc.psum_pool(name="tps", bufs=1))
        a_psum = ctx.enter_context(tc.psum_pool(name="aps", bufs=4))
        ctx.enter_context(tc.manual_schedule())

        rounds = [[0, 1], [2, 3]] + [list(range(s, s + ROUND)) for s in range(CHUNK, N_TILES, ROUND)]

        queue = [0, 1, 2, 3]
        bank_of = {}
        for run in [["w0"], ["w1"], ["w2"], ["w3"]] + rounds:
            taken = list(reversed(queue[: len(run)]))
            queue = queue[len(run) :] + taken
            for item, bank in zip(run, taken):
                bank_of[item] = bank

        ident = const.tile([P, P], F32, name="ident")
        make_identity(nc, ident[:])

        w_raw = []
        for wi, w_src in enumerate((weight_upper, weight_lower)):
            for h in range(2):
                wr = wraw_pool.tile([P, K], BF16, name="wraw%d" % (2 * wi + h), tag="wraw")
                nc.sync.dma_start(out=wr[:], in_=w_src[P * h : P * (h + 1), :])
                w_raw.append(wr)

        x_chunks = {}

        def load_chunk(c, pieces):
            xc = x_pool.tile([P, CHUNK * K], BF16, name="xc%d" % c, tag="xc")
            src = xf[CHUNK * P * c : CHUNK * P * (c + 1), :].rearrange("(p t) k -> p (t k)", t=CHUNK)
            step = CHUNK * K // pieces
            for i in range(pieces):
                nc.sync.dma_start(out=xc[:, step * i : step * (i + 1)], in_=src[:, step * i : step * (i + 1)])
            x_chunks[c] = xc

        load_chunk(0, 4)
        load_chunk(1, 2)
        for c in range(2, AHEAD):
            load_chunk(c, 1)

        warm_src = const.tile([P, WARM_COLS], BF16, name="warm_src")
        nc.vector.memset(warm_src[:], 0.0)
        warm_bank = a_psum.tile([P, WARM_COLS], F32, name="warm_bank", tag="acc")

        def keep_warm(n):
            for rep in range(n):
                nc.tensor.matmul(out=warm_bank[:], lhsT=warm_src[:, 0:P], rhs=warm_src[:], start=True, stop=True)

        keep_warm(WARM_FIRST)

        def transpose_words(bank, words):
            for c in range(4):
                nc.tensor.transpose(bank[:, c, :], words[:, P * c : P * (c + 1)], ident[:])

        w_codes = []
        w_scales = []
        for wi in range(2):
            wg = const.tile([P, 4 * PASSES * N_OUT], BF16, name="wg%d" % wi, align_bytes=64)
            wg_words = wg[:].bitcast(F32).rearrange("p (g n u) -> p g n u", g=PASSES, u=2)
            for h in range(2):
                wt = t_psum.tile([P, 4, P], F32, name="wt%d" % (2 * wi + h), tag="tb%d" % bank_of["w%d" % (2 * wi + h)])
                transpose_words(wt, w_raw[2 * wi + h][:].bitcast(F32))
                keep_warm(1)
                nc.scalar.copy(
                    out=wg_words[:, :, P * h : P * (h + 1), :],
                    in_=wt[:].rearrange("p (g u) r -> p g r u", u=2),
                )
            wc = const.tile([P, PASSES * N_OUT], U32, name="wc%d" % wi, align_bytes=64)
            ws = const.tile([P, PASSES * N_OUT], U8, name="ws%d" % wi, align_bytes=64)
            nc.vector.quantize_mx(out=wc[:].bitcast(FP8X4), scales=ws[:], in_=wg[:])
            w_codes.append(wc)
            w_scales.append(ws)

        grouped = {}
        x_codes = {}
        x_scales = {}
        acc = {}
        o_tiles = {}

        def transpose_tile(i):
            words = x_chunks[i // CHUNK][:].bitcast(F32)
            t = i % CHUNK
            xt = t_psum.tile([P, 4, P], F32, name="xt%d" % i, tag="tb%d" % bank_of[i])
            transpose_words(xt, words[:, K_WORDS * t : K_WORDS * (t + 1)])
            if i < WARM_TILES:
                keep_warm(1)
            gr = g_pool.tile([P, K], BF16, name="gr%d" % i, tag="gr", align_bytes=64)
            nc.scalar.copy(
                out=gr[:].bitcast(F32).rearrange("p (g r u) -> p g r u", g=PASSES, u=2),
                in_=xt[:].rearrange("p (g u) r -> p g r u", u=2),
            )
            grouped[i] = gr

        def quantise_tile(i):
            xcod = c_pool.tile([P, K // 4], U32, name="xcod%d" % i, tag="xcod", align_bytes=64)
            xsca = c_pool.tile([P, K // 4], U8, name="xsca%d" % i, tag="xsca", align_bytes=64)
            nc.vector.quantize_mx(out=xcod[:].bitcast(FP8X4), scales=xsca[:], in_=grouped[i][:])
            x_codes[i] = xcod
            x_scales[i] = xsca

        drained = {}

        def multiply_round(order, last):
            for n, i in enumerate(order):
                c = i // CHUNK
                alone = last and n >= len(order) - 2
                if n % 2 == 0 or alone:
                    acc[0] = a_psum.tile([P, 2, N_OUT], F32, name="acc%d" % i, tag="acc")
                if c not in o_tiles:
                    o_tiles[c] = o_pool.tile([P, CHUNK * N_OUT], F32, name="osb%d" % c, tag="osb")
                    drained[c] = 0
                n_pass = 0
                for g in range(PASSES):
                    for wi in range(2):
                        nc.tensor.matmul_mx(
                            out=acc[0][:, 0 if alone else i % 2, :],
                            lhsT=x_codes[i][:, P * g : P * (g + 1)].bitcast(FP8X4),
                            lhsT_scale=x_scales[i][:, P * g : P * (g + 1)],
                            rhs=w_codes[wi][:, N_OUT * g : N_OUT * (g + 1)].bitcast(FP8X4),
                            rhs_scale=w_scales[wi][:, N_OUT * g : N_OUT * (g + 1)],
                            start=(n_pass == 0),
                            stop=(n_pass == 2 * PASSES - 1),
                        )
                        n_pass += 1
                dst = of[CHUNK * P * c : CHUNK * P * (c + 1), :].rearrange("(p t) n -> p (t n)", t=CHUNK)
                if alone:
                    cols = slice(N_OUT * (i % CHUNK), N_OUT * (i % CHUNK + 1))
                    if n == len(order) - 2:
                        nc.scalar.copy(out=o_tiles[c][:, cols], in_=acc[0][:, 0, :])
                    else:
                        nc.vector.tensor_copy(out=o_tiles[c][:, cols], in_=acc[0][:, 0, :])
                    nc.sync.dma_start(out=dst[:, cols], in_=o_tiles[c][:, cols])
                elif n % 2 == 1:
                    b = (i // 2) % 2
                    cols = slice(2 * N_OUT * b, 2 * N_OUT * (b + 1))
                    nc.vector.tensor_copy(out=o_tiles[c][:, cols], in_=acc[0][:].rearrange("p h n -> p (h n)"))
                    drained[c] += 1
                    if last:
                        nc.sync.dma_start(out=dst[:, cols], in_=o_tiles[c][:, cols])
                    elif drained[c] == 2:
                        nc.sync.dma_start(out=dst, in_=o_tiles[c][:])
                        if c + AHEAD < N_CHUNKS:
                            load_chunk(c + AHEAD, 1)

        for k in range(-1, len(rounds)):
            if k + 1 < len(rounds):
                for i in rounds[k + 1]:
                    transpose_tile(i)
                for i in rounds[k + 1]:
                    quantise_tile(i)
            if k >= 0:
                order = rounds[k] if k < 2 else list(reversed(rounds[k]))
                multiply_round(order, k == len(rounds) - 1)
